import numpy as np
import ml_dtypes


def mxq(x, axis, fmt="e4m3"):
    dtype, down = {"e4m3": (ml_dtypes.float8_e4m3fn, 7), "e5m2": (ml_dtypes.float8_e5m2, 14)}[fmt]
    v = np.moveaxis(np.asarray(x, np.float32).astype(ml_dtypes.bfloat16).astype(np.float64), axis, -1)
    blocks = v.reshape(v.shape[:-1] + (-1, 32))
    amax = np.abs(blocks).max(-1, keepdims=True)
    byte = np.maximum(np.where(amax > 0, np.frexp(amax)[1] - 1 + 127, 0) - down, 1)
    scale = np.exp2(byte - 127.0)
    codes = (blocks / scale).astype(np.float32).astype(dtype).astype(np.float64)
    return np.moveaxis((codes * scale).reshape(v.shape), -1, axis)


WIDE = False


def mx_kscale(k):
    if not WIDE:
        return np.ones(k)
    levels = np.array([10, -10, 5, -5, 0])
    if k % 512:
        return np.exp2(np.random.permutation(np.resize(levels, k // 32))).repeat(32)
    a = np.empty((k // 512, 16))
    for p in range(k // 512):
        a[p, :8] = np.random.permutation(np.resize(levels, 8))
        for g in range(8):
            far = levels[np.abs(levels - a[p, g]) >= 10]
            a[p, g + 8] = far[np.random.randint(len(far))]
    return np.exp2(a.ravel()).repeat(32)


BF16 = ml_dtypes.bfloat16


def bf(x):
    return np.asarray(x, np.float32).astype(BF16)


def f64(x):
    return np.asarray(x).astype(np.float64)


B, IDIM, HDIM, ODIM, S, DEPTH, NACT, NTOP = 1024, 512, 1024, 512, 128, 32, 3, 2


def sigmoid(v):
    return 1.0 / (1.0 + np.exp(-v))


def setup_inputs():
    s, t = mx_kscale(IDIM), mx_kscale(HDIM)
    return {"x": bf(np.random.standard_normal((B, IDIM)) * s),
            "hidden": bf(np.random.standard_normal((B, HDIM)) * t),
            "stack_top": bf(np.random.standard_normal((B, NTOP, S))),
            "Wi": bf(np.random.standard_normal((HDIM, IDIM)) * 0.7 / np.sqrt(IDIM) / s),
            "bi": bf(np.random.standard_normal(HDIM) * 0.2),
            "Wh": bf(np.random.standard_normal((HDIM, HDIM)) * 0.7 / np.sqrt(HDIM) / t),
            "bh": bf(np.random.standard_normal(HDIM) * 0.2),
            "W0": bf(np.random.standard_normal((HDIM, S)) * 0.5 / np.sqrt(S)),
            "b0": bf(np.random.standard_normal(HDIM) * 0.2),
            "W1": bf(np.random.standard_normal((HDIM, S)) * 0.5 / np.sqrt(S)),
            "b1": bf(np.random.standard_normal(HDIM) * 0.2)}


def reference(x, hidden, stack_top, Wi, bi, Wh, bh, W0, b0, W1, b1):
    pre = ((mxq(f64(x), 1, "e4m3") @ mxq(f64(Wi), 1, "e4m3").T) + f64(bi)
           + (mxq(f64(hidden), 1, "e4m3") @ mxq(f64(Wh), 1, "e4m3").T) + f64(bh)
           + f64(stack_top)[:, 0] @ f64(W0).T + f64(b0)
           + f64(stack_top)[:, 1] @ f64(W1).T + f64(b1))
    return sigmoid(pre)

@@ -1,0 +1,250 @@
+from contextlib import ExitStack
+
+import concourse.mybir as mybir
+from concourse.masks import make_identity
+
+F32 = mybir.dt.float32
+BF16 = mybir.dt.bfloat16
+U32 = mybir.dt.uint32
+U8 = mybir.dt.uint8
+FP8X4 = mybir.dt.float8_e4m3fn_x4
+ADD = mybir.AluOpType.add
+SIGMOID = mybir.ActivationFunctionType.Sigmoid
+
+P = 128
+B, IDIM, HDIM, S = 1024, 512, 1024, 128
+NB = B // P
+PASSES = 3
+ST_SLOTS = ((0, 1), (2, 3, 4, 5), (6, 7))
+FLOPS = 2 * B * HDIM * (IDIM + HDIM + 2 * S)
+
+
+def tile_stackrnn_pa_kernel(tc, x, hidden, stack_top, Wi, bi, Wh, bh, W0, b0, W1, b1, out):
+    nc = tc.nc
+    with ExitStack() as ctx:
+        keep = ctx.enter_context(tc.tile_pool(name="keep", bufs=1))
+        psum = ctx.enter_context(tc.psum_pool(name="psum", bufs=8))
+        ctx.enter_context(tc.manual_schedule())
+
+        x_sb = keep.tile([P, NB * IDIM], BF16)
+        h_sb = keep.tile([P, NB * HDIM], BF16)
+        st_sb = keep.tile([P, NB * 2 * S], BF16)
+        wi_sb = keep.tile([P, 8 * IDIM], BF16)
+        wh_sb = keep.tile([P, 8 * HDIM], BF16)
+        w01_sb = keep.tile([P, 2 * 4 * 2 * S], BF16)
+        bias_rows = keep.tile([P, HDIM], BF16)
+        ones = keep.tile([P, P], BF16)
+        junk = keep.tile([P, 512], BF16)
+        ident_f = keep.tile([P, P], F32)
+        warm = keep.tile([P, 1], F32)
+        stT = keep.tile([P, NB * P * 2], BF16)
+        w01T = keep.tile([P, HDIM * 2], BF16)
+        bias_bc = keep.tile([P, HDIM], F32)
+        a_codes = keep.tile([P, PASSES, B], U32, align_bytes=64)
+        a_scales = keep.tile([P, PASSES, B], U8, align_bytes=64)
+        w_codes = keep.tile([P, PASSES, HDIM], U32, align_bytes=64)
+        w_scales = keep.tile([P, PASSES, HDIM], U8, align_bytes=64)
+        pre = keep.tile([P, NB, HDIM], F32)
+
+        nc.vector.memset(ones[:], 1.0)
+        nc.vector.memset(junk[:], 0.0)
+        nc.vector.memset(bias_rows[:], 0.0)
+        nc.vector.memset(warm[:], 0.0)
+        make_identity(nc, ident_f[:])
+
+        st_v = stack_top.rearrange("(p t) s k -> p (t s k)", t=NB)
+        w0_v = W0.rearrange("(n t p) k -> p n t k", n=2, t=4)
+        w1_v = W1.rearrange("(n t p) k -> p n t k", n=2, t=4)
+        w01_t = w01_sb[:].rearrange("p (n t s k) -> p n t s k", n=2, t=4, s=2)
+        x_v = x.rearrange("(p t) k -> p (t k)", t=NB)
+        h_v = hidden.rearrange("(p t) k -> p (t k)", t=NB)
+        wi_v = Wi.rearrange("(g p t) k -> p g (t k)", g=4, t=2)
+        wh_v = Wh.rearrange("(g p t) k -> p g (t k)", g=4, t=2)
+        wi_t = wi_sb[:].rearrange("p (g c) -> p g c", g=4)
+
+        nc.sync.dma_start(out=w01_t[:, 0, :, 0, :], in_=w0_v[:, 0])
+        nc.sync.dma_start(out=w01_t[:, 0, :, 1, :], in_=w1_v[:, 0])
+        nc.sync.dma_start(out=st_sb[:, 0:512], in_=st_v[:, 0:512])
+        nc.sync.dma_start(out=st_sb[:, 512:2048], in_=st_v[:, 512:2048])
+        for r, b_vec in enumerate((bi, bh, b0, b1)):
+            nc.scalar.dma_start(out=bias_rows[r : r + 1, :], in_=b_vec.rearrange("(o n) -> o n", o=1))
+        nc.scalar.activation(out=warm[:], in_=warm[:], func=SIGMOID)
+        nc.sync.dma_start(out=w01_t[:, 1, :, 0, :], in_=w0_v[:, 1])
+        nc.sync.dma_start(out=w01_t[:, 1, :, 1, :], in_=w1_v[:, 1])
+        for gg in range(2):
+            nc.sync.dma_start(out=wi_t[:, 2 * gg : 2 * gg + 2, :], in_=wi_v[:, 2 * gg : 2 * gg + 2, :])
+            for g in (2 * gg, 2 * gg + 1):
+                nc.sync.dma_start(out=wh_sb[:, g * 2048 : (g + 1) * 2048], in_=wh_v[:, g, :])
+        for hh in range(2):
+            nc.sync.dma_start(out=x_sb[:, hh * 2048 : (hh + 1) * 2048], in_=x_v[:, hh * 2048 : (hh + 1) * 2048])
+            for pr in (2 * hh, 2 * hh + 1):
+                nc.sync.dma_start(out=h_sb[:, pr * 2048 : (pr + 1) * 2048], in_=h_v[:, pr * 2048 : (pr + 1) * 2048])
+
+        words = {"s": st_sb[:].bitcast(F32), "v": w01_sb[:].bitcast(F32)}
+        mx_words = {("a", 0): x_sb[:].bitcast(F32), ("a", 1): h_sb[:].bitcast(F32), ("w", 0): wi_sb[:].bitcast(F32), ("w", 1): wh_sb[:].bitcast(F32)}
+        stT_w = stT[:].bitcast(F32)
+        w01T_w = w01T[:].bitcast(F32)
+        stT_e = stT[:].rearrange("p (t j e) -> p t j e", t=NB, e=2)
+        w01T_e = w01T[:].rearrange("p (n h e) -> p n h e", n=2, e=2)
+        out_v = out.rearrange("(p t) h -> p t h", t=NB)
+        grouped = {}
+        banks = {}
+
+        def sources(kind, c, q):
+            if kind == "s":
+                return [words[kind][:, t * P : (t + 1) * P] for t in ST_SLOTS[q]]
+            if kind == "v":
+                return [words[kind][:, (4 * q + i) * P : (4 * q + i + 1) * P] for i in range(4)]
+            src = mx_words[(kind, min(c, 1))]
+            row_words = IDIM // 2 if c == 0 else HDIM // 2
+            off = 0 if c == 0 else (c - 1) * 256
+            return [
+                src[:, (2 * q + r) * row_words + off + u : (2 * q + r) * row_words + off + 2 * P : 2]
+                for r in range(2)
+                for u in range(2)
+            ]
+
+        def transposes(job, first, last):
+            if first == 0:
+                banks[job] = psum.tile([P, 512], F32, tag="bank", name="tbank")
+            srcs = sources(*job)
+            for i in range(first, last):
+                nc.tensor.transpose(banks[job][:, i * P : (i + 1) * P], srcs[i], ident_f[:])
+
+        def copy_out(job, on_vector=False):
+            kind, c, q = job
+            bank = banks[job]
+            if kind == "s":
+                slots = ST_SLOTS[q]
+                dst, src = stT_w[:, slots[0] * P : (slots[-1] + 1) * P], bank[:, 0 : len(slots) * P]
+            elif kind == "v":
+                dst, src = w01T_w[:, q * 512 : (q + 1) * 512], bank[:]
+            else:
+                grouped[job] = keep.tile([P, 1024], BF16, align_bytes=64, name="grp_%s%d%d" % job)
+                gw = grouped[job][:].bitcast(F32)
+                if kind == "a":
+                    dst = gw.rearrange("p (r j u) -> p r j u", r=2, u=2)
+                    src = bank[:].rearrange("p (r u j) -> p r j u", r=2, u=2)
+                else:
+                    dst = gw.rearrange("p (j r u) -> p j r u", r=2, u=2)
+                    src = bank[:].rearrange("p (r u j) -> p j r u", r=2, u=2)
+            if on_vector:
+                nc.vector.tensor_copy(out=dst, in_=src)
+            else:
+                nc.scalar.copy(out=dst, in_=src)
+
+        def quantise(job):
+            kind, c, q = job
+            codes, scales = (a_codes, a_scales) if kind == "a" else (w_codes, w_scales)
+            cols = slice(q * 256, (q + 1) * 256)
+            nc.vector.quantize_mx(out=codes[:, c, cols].bitcast(FP8X4), scales=scales[:, c, cols], in_=grouped[job][:])
+
+        def plain_matmul(group, e):
+            m, n = group
+            if e == 0:
+                banks[group] = psum.tile([P, 512], F32, tag="bank", name="pbank")
+            nc.tensor.matmul(banks[group][:], lhsT=stT_e[:, m, :, e], rhs=w01T_e[:, n, :, e], start=(e == 0), stop=(e == 1))
+
+        def add_bias(group):
+            m, n = group
+            cols = slice(n * 512, (n + 1) * 512)
+            nc.vector.tensor_tensor(out=pre[:, m, cols], in0=banks[group][:], in1=bias_bc[:, cols], op=ADD)
+
+        def bank_alone(job, on_vector=False):
+            transposes(job, 0, len(sources(*job)))
+            copy_out(job, on_vector)
+
+        def woven(group, job, with_bias=True):
+            plain_matmul(group, 0)
+            transposes(job, 0, 2)
+            plain_matmul(group, 1)
+            transposes(job, 2, len(sources(*job)))
+            copy_out(job)
+            if with_bias:
+                add_bias(group)
+
+        def warm_up(count):
+            for i in range(count):
+                nc.tensor.matmul(warm_bank[:], lhsT=ones[:], rhs=junk[:], start=True, stop=True)
+
+        def finish(m, first_col, last_col):
+            cols = slice(first_col, last_col)
+            nc.scalar.activation(out=pre[:, m, cols], in_=pre[:, m, cols], func=SIGMOID)
+            nc.sync.dma_start(out=out_v[:, m, cols], in_=pre[:, m, cols])
+
+        def mx_group(m, n, pieces=0):
+            bank = psum.tile([P, 512], F32, tag="bank", name="mbank")
+            rows = slice(m * P, (m + 1) * P)
+            cols = slice(n * 512, (n + 1) * 512)
+            for c in range(PASSES):
+                nc.tensor.matmul_mx(
+                    out=bank[:],
+                    lhsT=a_codes[:, c, rows].bitcast(FP8X4),
+                    lhsT_scale=a_scales[:, c, rows],
+                    rhs=w_codes[:, c, cols].bitcast(FP8X4),
+                    rhs_scale=w_scales[:, c, cols],
+                    start=(c == 0),
+                    stop=(c == PASSES - 1),
+                )
+            width = 512 // max(pieces, 1)
+            for i in range(max(pieces, 1)):
+                part = slice(n * 512 + i * width, n * 512 + (i + 1) * width)
+                nc.vector.tensor_tensor(out=pre[:, m, part], in0=bank[:, i * width : (i + 1) * width], in1=pre[:, m, part], op=ADD)
+                if pieces > 0:
+                    finish(m, n * 512 + i * width, n * 512 + (i + 1) * width)
+
+        warm_bank = psum.tile([P, 512], F32, tag="bank", name="wbank")
+        warm_up(6)
+        bank_alone(("v", 0, 0))
+        bank_alone(("s", 0, 0), on_vector=True)
+        warm_up(1)
+        woven((0, 0), ("s", 0, 1), with_bias=False)
+        woven((1, 0), ("s", 0, 2), with_bias=False)
+        bias_banks = []
+        for n in range(2):
+            bias_banks.append(psum.tile([P, 512], F32, tag="bank", name="bbank"))
+            nc.tensor.matmul(bias_banks[n][:], lhsT=ones[:], rhs=bias_rows[:, n * 512 : (n + 1) * 512], start=True, stop=True)
+        nc.vector.tensor_copy(out=bias_bc[:, 0:512], in_=bias_banks[0][:])
+        nc.scalar.copy(out=bias_bc[:, 512:1024], in_=bias_banks[1][:])
+        add_bias((0, 0))
+        add_bias((1, 0))
+        woven((2, 0), ("v", 0, 1))
+
+        groups = [(3, 0), (4, 0), (5, 0)] + [(m, 1) for m in range(6)] + [(6, 0), (6, 1), (7, 0), (7, 1)]
+        chunks = []
+        for kind in ("w", "a"):
+            for hh in range(2):
+                chunks.append([(kind, 0, 2 * hh), (kind, 0, 2 * hh + 1)])
+                for q in (2 * hh, 2 * hh + 1):
+                    chunks.append([(kind, 1, q), (kind, 2, q)])
+        EARLY = 10
+        plain_matmul(groups[0], 0)
+        plain_matmul(groups[0], 1)
+        add_bias(groups[0])
+        gi = 1
+        for i in range(EARLY):
+            job_a, job_b = chunks[i]
+            bank_alone(job_a)
+            quantise(job_a)
+            woven(groups[gi], job_b)
+            gi += 1
+            quantise(job_b)
+        for m in range(4):
+            mx_group(m, 0)
+            mx_group(m, 1)
+            if m < 3:
+                finish(m, 0, HDIM)
+        for i in range(EARLY, len(chunks)):
+            job_a, job_b = chunks[i]
+            bank_alone(job_a)
+            woven(groups[gi], job_b)
+            gi += 1
+            quantise(job_a)
+            quantise(job_b)
+        finish(3, 0, HDIM)
+        mx_group(4, 0)
+        mx_group(4, 1)
+        finish(4, 0, HDIM)
+        for m in range(5, 8):
+            mx_group(m, 0, pieces=1)
+            mx_group(m, 1, pieces=(2 if m == 7 else 1))

@@ -45,6 +45,8 @@ def tile_stackrnn_pa_kernel(tc, x, hidden, stack_top, Wi, bi, Wh, bh, W0, b0, W1
         w_codes = keep.tile([P, PASSES, HDIM], U32, align_bytes=64)
         w_scales = keep.tile([P, PASSES, HDIM], U8, align_bytes=64)
         pre = keep.tile([P, NB, HDIM], F32)
+        xp_sb = keep.tile([P, NB * IDIM // 2], F32)
+        hp_sb = keep.tile([P, NB * HDIM // 2], F32)
 
         nc.vector.memset(ones[:], 1.0)
         nc.vector.memset(junk[:], 0.0)
@@ -81,7 +83,8 @@ def tile_stackrnn_pa_kernel(tc, x, hidden, stack_top, Wi, bi, Wh, bh, W0, b0, W1
                 nc.sync.dma_start(out=h_sb[:, pr * 2048 : (pr + 1) * 2048], in_=h_v[:, pr * 2048 : (pr + 1) * 2048])
 
         words = {"s": st_sb[:].bitcast(F32), "v": w01_sb[:].bitcast(F32)}
-        mx_words = {("a", 0): x_sb[:].bitcast(F32), ("a", 1): h_sb[:].bitcast(F32), ("w", 0): wi_sb[:].bitcast(F32), ("w", 1): wh_sb[:].bitcast(F32)}
+        mx_words = {("a", 0): xp_sb[:], ("a", 1): hp_sb[:], ("w", 0): wi_sb[:].bitcast(F32), ("w", 1): wh_sb[:].bitcast(F32)}
+        raw_words = (x_sb[:].bitcast(F32), h_sb[:].bitcast(F32))
         stT_w = stT[:].bitcast(F32)
         w01T_w = w01T[:].bitcast(F32)
         stT_e = stT[:].rearrange("p (t j e) -> p t j e", t=NB, e=2)
@@ -98,11 +101,20 @@ def tile_stackrnn_pa_kernel(tc, x, hidden, stack_top, Wi, bi, Wh, bh, W0, b0, W1
             src = mx_words[(kind, min(c, 1))]
             row_words = IDIM // 2 if c == 0 else HDIM // 2
             off = 0 if c == 0 else (c - 1) * 256
-            return [
-                src[:, (2 * q + r) * row_words + off + u : (2 * q + r) * row_words + off + 2 * P : 2]
-                for r in range(2)
-                for u in range(2)
-            ]
+            first = [(2 * q + r) * row_words + off for r in range(2)]
+            if kind == "a":
+                return [src[:, f + u * P : f + (u + 1) * P] for f in first for u in range(2)]
+            return [src[:, f + u : f + 2 * P : 2] for f in first for u in range(2)]
+
+        def permute(chunk):
+            big = min(chunk[0][1], 1)
+            row_words = HDIM // 2 if big else IDIM // 2
+            for q in sorted(set(job[2] for job in chunk)):
+                words_of = slice(2 * q * row_words, (2 * q + 2) * row_words)
+                nc.vector.tensor_copy(
+                    out=mx_words[("a", big)][:, words_of].rearrange("p (r u i) -> p r u i", u=2, i=P),
+                    in_=raw_words[big][:, words_of].rearrange("p (r i u) -> p r u i", u=2, i=P),
+                )
 
         def transposes(job, first, last):
             if first == 0:
@@ -225,6 +237,8 @@ def tile_stackrnn_pa_kernel(tc, x, hidden, stack_top, Wi, bi, Wh, bh, W0, b0, W1
         for i in range(EARLY):
             job_a, job_b = chunks[i]
             bank_alone(job_a)
+            if chunks[i + 2][0][0] == "a":
+                permute(chunks[i + 2])
             quantise(job_a)
             woven(groups[gi], job_b)
             gi += 1

@@ -103,7 +103,9 @@ def tile_stackrnn_pa_kernel(tc, x, hidden, stack_top, Wi, bi, Wh, bh, W0, b0, W1
             off = 0 if c == 0 else (c - 1) * 256
             first = [(2 * q + r) * row_words + off for r in range(2)]
             if kind == "a":
-                return [src[:, f + u * P : f + (u + 1) * P] for f in first for u in range(2)]
+                base = 2 * q * row_words
+                first = [base + r * row_words // 2 + off // 2 for r in range(2)]
+                return [src[:, f + u * row_words : f + u * row_words + P] for f in first for u in range(2)]
             return [src[:, f + u : f + 2 * P : 2] for f in first for u in range(2)]
 
         def permute(chunk):
@@ -112,8 +114,8 @@ def tile_stackrnn_pa_kernel(tc, x, hidden, stack_top, Wi, bi, Wh, bh, W0, b0, W1
             for q in sorted(set(job[2] for job in chunk)):
                 words_of = slice(2 * q * row_words, (2 * q + 2) * row_words)
                 nc.vector.tensor_copy(
-                    out=mx_words[("a", big)][:, words_of].rearrange("p (r u i) -> p r u i", u=2, i=P),
-                    in_=raw_words[big][:, words_of].rearrange("p (r i u) -> p r u i", u=2, i=P),
+                    out=mx_words[("a", big)][:, words_of].rearrange("p (u b i) -> p b u i", u=2, i=4),
+                    in_=raw_words[big][:, words_of].rearrange("p (b i u) -> p b u i", u=2, i=4),
                 )
 
         def transposes(job, first, last):
@@ -229,7 +231,7 @@ def tile_stackrnn_pa_kernel(tc, x, hidden, stack_top, Wi, bi, Wh, bh, W0, b0, W1
                 chunks.append([(kind, 0, 2 * hh), (kind, 0, 2 * hh + 1)])
                 for q in (2 * hh, 2 * hh + 1):
                     chunks.append([(kind, 1, q), (kind, 2, q)])
-        EARLY = 10
+        EARLY = 9
         plain_matmul(groups[0], 0)
         plain_matmul(groups[0], 1)
         add_bias(groups[0])
@@ -237,7 +239,7 @@ def tile_stackrnn_pa_kernel(tc, x, hidden, stack_top, Wi, bi, Wh, bh, W0, b0, W1
         for i in range(EARLY):
             job_a, job_b = chunks[i]
             bank_alone(job_a)
-            if chunks[i + 2][0][0] == "a":
+            if i + 2 < EARLY and chunks[i + 2][0][0] == "a":
                 permute(chunks[i + 2])
             quantise(job_a)
             woven(groups[gi], job_b)
@@ -247,6 +249,7 @@ def tile_stackrnn_pa_kernel(tc, x, hidden, stack_top, Wi, bi, Wh, bh, W0, b0, W1
             mx_group(m, 0)
             mx_group(m, 1)
             if m < 3:
+                permute(chunks[EARLY + m])
                 finish(m, 0, HDIM)
         for i in range(EARLY, len(chunks)):
             job_a, job_b = chunks[i]

@@ -168,12 +168,9 @@ def tile_stackrnn_pa_kernel(tc, x, hidden, stack_top, Wi, bi, Wh, bh, W0, b0, W1
             transposes(job, 0, len(sources(*job)))
             copy_out(job, on_vector)
 
-        def woven(group, job, with_bias=True):
+        def plain_group(group, with_bias=True):
             plain_matmul(group, 0)
-            transposes(job, 0, 2)
             plain_matmul(group, 1)
-            transposes(job, 2, len(sources(*job)))
-            copy_out(job)
             if with_bias:
                 add_bias(group)
 
@@ -212,8 +209,10 @@ def tile_stackrnn_pa_kernel(tc, x, hidden, stack_top, Wi, bi, Wh, bh, W0, b0, W1
         bank_alone(("v", 0, 0))
         bank_alone(("s", 0, 0), on_vector=True)
         warm_up(1)
-        woven((0, 0), ("s", 0, 1), with_bias=False)
-        woven((1, 0), ("s", 0, 2), with_bias=False)
+        bank_alone(("s", 0, 1))
+        plain_group((0, 0), with_bias=False)
+        bank_alone(("s", 0, 2))
+        plain_group((1, 0), with_bias=False)
         bias_banks = []
         for n in range(2):
             bias_banks.append(psum.tile([P, 512], F32, tag="bank", name="bbank"))
@@ -222,7 +221,8 @@ def tile_stackrnn_pa_kernel(tc, x, hidden, stack_top, Wi, bi, Wh, bh, W0, b0, W1
         nc.scalar.copy(out=bias_bc[:, 512:1024], in_=bias_banks[1][:])
         add_bias((0, 0))
         add_bias((1, 0))
-        woven((2, 0), ("v", 0, 1))
+        bank_alone(("v", 0, 1))
+        plain_group((2, 0))
 
         groups = [(3, 0), (4, 0), (5, 0)] + [(m, 1) for m in range(6)] + [(6, 0), (6, 1), (7, 0), (7, 1)]
         chunks = []
@@ -232,17 +232,16 @@ def tile_stackrnn_pa_kernel(tc, x, hidden, stack_top, Wi, bi, Wh, bh, W0, b0, W1
                 for q in (2 * hh, 2 * hh + 1):
                     chunks.append([(kind, 1, q), (kind, 2, q)])
         EARLY = 9
-        plain_matmul(groups[0], 0)
-        plain_matmul(groups[0], 1)
-        add_bias(groups[0])
+        plain_group(groups[0])
         gi = 1
         for i in range(EARLY):
             job_a, job_b = chunks[i]
             bank_alone(job_a)
             if i + 2 < EARLY and chunks[i + 2][0][0] == "a":
                 permute(chunks[i + 2])
+            bank_alone(job_b)
             quantise(job_a)
-            woven(groups[gi], job_b)
+            plain_group(groups[gi])
             gi += 1
             quantise(job_b)
         for m in range(4):
@@ -254,7 +253,8 @@ def tile_stackrnn_pa_kernel(tc, x, hidden, stack_top, Wi, bi, Wh, bh, W0, b0, W1
         for i in range(EARLY, len(chunks)):
             job_a, job_b = chunks[i]
             bank_alone(job_a)
-            woven(groups[gi], job_b)
+            bank_alone(job_b)
+            plain_group(groups[gi])
             gi += 1
             quantise(job_a)
             quantise(job_b)

@@ -31,6 +31,7 @@ def tile_stackrnn_pa_kernel(tc, x, hidden, stack_top, Wi, bi, Wh, bh, W0, b0, W1
         st_sb = keep.tile([P, NB * 2 * S], BF16)
         wi_sb = keep.tile([P, 8 * IDIM], BF16)
         wh_sb = keep.tile([P, 8 * HDIM], BF16)
+        w01_raw = keep.tile([P, 2 * 2 * 4 * S], BF16)
         w01_sb = keep.tile([P, 2 * 4 * 2 * S], BF16)
         bias_rows = keep.tile([P, HDIM], BF16)
         ones = keep.tile([P, P], BF16)
@@ -55,24 +56,24 @@ def tile_stackrnn_pa_kernel(tc, x, hidden, stack_top, Wi, bi, Wh, bh, W0, b0, W1
         make_identity(nc, ident_f[:])
 
         st_v = stack_top.rearrange("(p t) s k -> p (t s k)", t=NB)
-        w0_v = W0.rearrange("(n t p) k -> p n t k", n=2, t=4)
-        w1_v = W1.rearrange("(n t p) k -> p n t k", n=2, t=4)
-        w01_t = w01_sb[:].rearrange("p (n t s k) -> p n t s k", n=2, t=4, s=2)
+        w0_v = W0.rearrange("(n p t) k -> p n (t k)", n=2, t=4)
+        w1_v = W1.rearrange("(n p t) k -> p n (t k)", n=2, t=4)
+        w01_r = w01_raw[:].rearrange("p (n s c) -> p n s c", n=2, s=2)
         x_v = x.rearrange("(p t) k -> p (t k)", t=NB)
         h_v = hidden.rearrange("(p t) k -> p (t k)", t=NB)
         wi_v = Wi.rearrange("(g p t) k -> p g (t k)", g=4, t=2)
         wh_v = Wh.rearrange("(g p t) k -> p g (t k)", g=4, t=2)
         wi_t = wi_sb[:].rearrange("p (g c) -> p g c", g=4)
 
-        nc.sync.dma_start(out=w01_t[:, 0, :, 0, :], in_=w0_v[:, 0])
-        nc.sync.dma_start(out=w01_t[:, 0, :, 1, :], in_=w1_v[:, 0])
+        nc.sync.dma_start(out=w01_r[:, 0, 0, :], in_=w0_v[:, 0, :])
+        nc.sync.dma_start(out=w01_r[:, 0, 1, :], in_=w1_v[:, 0, :])
         nc.sync.dma_start(out=st_sb[:, 0:512], in_=st_v[:, 0:512])
         nc.sync.dma_start(out=st_sb[:, 512:2048], in_=st_v[:, 512:2048])
         for r, b_vec in enumerate((bi, bh, b0, b1)):
             nc.scalar.dma_start(out=bias_rows[r : r + 1, :], in_=b_vec.rearrange("(o n) -> o n", o=1))
         nc.scalar.activation(out=warm[:], in_=warm[:], func=SIGMOID)
-        nc.sync.dma_start(out=w01_t[:, 1, :, 0, :], in_=w0_v[:, 1])
-        nc.sync.dma_start(out=w01_t[:, 1, :, 1, :], in_=w1_v[:, 1])
+        nc.sync.dma_start(out=w01_r[:, 1, 0, :], in_=w0_v[:, 1, :])
+        nc.sync.dma_start(out=w01_r[:, 1, 1, :], in_=w1_v[:, 1, :])
         for gg in range(2):
             nc.sync.dma_start(out=wi_t[:, 2 * gg : 2 * gg + 2, :], in_=wi_v[:, 2 * gg : 2 * gg + 2, :])
             for g in (2 * gg, 2 * gg + 1):
@@ -91,6 +92,7 @@ def tile_stackrnn_pa_kernel(tc, x, hidden, stack_top, Wi, bi, Wh, bh, W0, b0, W1
         w01T_e = w01T[:].rearrange("p (n h e) -> p n h e", n=2, e=2)
         out_v = out.rearrange("(p t) h -> p t h", t=NB)
         grouped = {}
+        permuted = set()
         banks = {}
 
         def sources(kind, c, q):
@@ -102,21 +104,26 @@ def tile_stackrnn_pa_kernel(tc, x, hidden, stack_top, Wi, bi, Wh, bh, W0, b0, W1
             row_words = IDIM // 2 if c == 0 else HDIM // 2
             off = 0 if c == 0 else (c - 1) * 256
             first = [(2 * q + r) * row_words + off for r in range(2)]
-            if kind == "a":
+            if kind == "a" and (min(c, 1), q) in permuted:
                 base = 2 * q * row_words
                 first = [base + r * row_words // 2 + off // 2 for r in range(2)]
                 return [src[:, f + u * row_words : f + u * row_words + P] for f in first for u in range(2)]
+            if kind == "a":
+                src = raw_words[min(c, 1)]
             return [src[:, f + u : f + 2 * P : 2] for f in first for u in range(2)]
 
-        def permute(chunk):
+        def permute(chunk, on_vector=True):
             big = min(chunk[0][1], 1)
             row_words = HDIM // 2 if big else IDIM // 2
             for q in sorted(set(job[2] for job in chunk)):
+                permuted.add((big, q))
                 words_of = slice(2 * q * row_words, (2 * q + 2) * row_words)
-                nc.vector.tensor_copy(
-                    out=mx_words[("a", big)][:, words_of].rearrange("p (u b i) -> p b u i", u=2, i=4),
-                    in_=raw_words[big][:, words_of].rearrange("p (b i u) -> p b u i", u=2, i=4),
-                )
+                dst = mx_words[("a", big)][:, words_of].rearrange("p (u b i) -> p b u i", u=2, i=4)
+                src = raw_words[big][:, words_of].rearrange("p (b i u) -> p b u i", u=2, i=4)
+                if on_vector:
+                    nc.vector.tensor_copy(out=dst, in_=src)
+                else:
+                    nc.scalar.copy(out=dst, in_=src)
 
         def transposes(job, first, last):
             if first == 0:
@@ -132,7 +139,8 @@ def tile_stackrnn_pa_kernel(tc, x, hidden, stack_top, Wi, bi, Wh, bh, W0, b0, W1
                 slots = ST_SLOTS[q]
                 dst, src = stT_w[:, slots[0] * P : (slots[-1] + 1) * P], bank[:, 0 : len(slots) * P]
             elif kind == "v":
-                dst, src = w01T_w[:, q * 512 : (q + 1) * 512], bank[:]
+                dst = w01T_w[:, q * 512 : (q + 1) * 512].rearrange("p (j t) -> p j t", t=4)
+                src = bank[:].rearrange("p (t j) -> p j t", t=4)
             else:
                 grouped[job] = keep.tile([P, 1024], BF16, align_bytes=64, name="grp_%s%d%d" % job)
                 gw = grouped[job][:].bitcast(F32)
@@ -146,6 +154,11 @@ def tile_stackrnn_pa_kernel(tc, x, hidden, stack_top, Wi, bi, Wh, bh, W0, b0, W1
                 nc.vector.tensor_copy(out=dst, in_=src)
             else:
                 nc.scalar.copy(out=dst, in_=src)
+
+        def pair_rows(n):
+            dst = words["v"][:, n * 512 : (n + 1) * 512].rearrange("p (t s w) -> p s t w", t=4, s=2)
+            src = w01_raw[:].bitcast(F32)[:, n * 512 : (n + 1) * 512].rearrange("p (s t w) -> p s t w", s=2, t=4)
+            nc.vector.tensor_copy(out=dst, in_=src)
 
         def quantise(job):
             kind, c, q = job
@@ -183,13 +196,13 @@ def tile_stackrnn_pa_kernel(tc, x, hidden, stack_top, Wi, bi, Wh, bh, W0, b0, W1
             nc.scalar.activation(out=pre[:, m, cols], in_=pre[:, m, cols], func=SIGMOID)
             nc.sync.dma_start(out=out_v[:, m, cols], in_=pre[:, m, cols])
 
-        def mx_group(m, n, pieces=0):
+        def mx_group(m, first_col, width=512, pieces=0):
             bank = psum.tile([P, 512], F32, tag="bank", name="mbank")
             rows = slice(m * P, (m + 1) * P)
-            cols = slice(n * 512, (n + 1) * 512)
+            cols = slice(first_col, first_col + width)
             for c in range(PASSES):
                 nc.tensor.matmul_mx(
-                    out=bank[:],
+                    out=bank[:, 0:width],
                     lhsT=a_codes[:, c, rows].bitcast(FP8X4),
                     lhsT_scale=a_scales[:, c, rows],
                     rhs=w_codes[:, c, cols].bitcast(FP8X4),
@@ -197,18 +210,20 @@ def tile_stackrnn_pa_kernel(tc, x, hidden, stack_top, Wi, bi, Wh, bh, W0, b0, W1
                     start=(c == 0),
                     stop=(c == PASSES - 1),
                 )
-            width = 512 // max(pieces, 1)
+            step = width // max(pieces, 1)
             for i in range(max(pieces, 1)):
-                part = slice(n * 512 + i * width, n * 512 + (i + 1) * width)
-                nc.vector.tensor_tensor(out=pre[:, m, part], in0=bank[:, i * width : (i + 1) * width], in1=pre[:, m, part], op=ADD)
+                part = slice(first_col + i * step, first_col + (i + 1) * step)
+                nc.vector.tensor_tensor(out=pre[:, m, part], in0=bank[:, i * step : (i + 1) * step], in1=pre[:, m, part], op=ADD)
                 if pieces > 0:
-                    finish(m, n * 512 + i * width, n * 512 + (i + 1) * width)
+                    finish(m, part.start, part.stop)
 
         warm_bank = psum.tile([P, 512], F32, tag="bank", name="wbank")
         warm_up(6)
+        pair_rows(0)
         bank_alone(("v", 0, 0))
         bank_alone(("s", 0, 0), on_vector=True)
         warm_up(1)
+        pair_rows(1)
         bank_alone(("s", 0, 1))
         plain_group((0, 0), with_bias=False)
         bank_alone(("s", 0, 2))
@@ -237,31 +252,39 @@ def tile_stackrnn_pa_kernel(tc, x, hidden, stack_top, Wi, bi, Wh, bh, W0, b0, W1
         for i in range(EARLY):
             job_a, job_b = chunks[i]
             bank_alone(job_a)
-            if i + 2 < EARLY and chunks[i + 2][0][0] == "a":
+            if i + 2 in (7, 8):
                 permute(chunks[i + 2])
             bank_alone(job_b)
             quantise(job_a)
             plain_group(groups[gi])
             gi += 1
             quantise(job_b)
+        permute(chunks[9], on_vector=False)
         for m in range(4):
             mx_group(m, 0)
-            mx_group(m, 1)
+            mx_group(m, 512)
             if m < 3:
-                permute(chunks[EARLY + m])
+                if m < 2:
+                    permute(chunks[10 + m])
                 finish(m, 0, HDIM)
         for i in range(EARLY, len(chunks)):
             job_a, job_b = chunks[i]
             bank_alone(job_a)
             bank_alone(job_b)
+            if i == EARLY + 1:
+                finish(3, 0, HDIM)
             plain_group(groups[gi])
             gi += 1
-            quantise(job_a)
-            quantise(job_b)
-        finish(3, 0, HDIM)
-        mx_group(4, 0)
-        mx_group(4, 1)
-        finish(4, 0, HDIM)
-        for m in range(5, 8):
+            if i < len(chunks) - 1:
+                quantise(job_a)
+                quantise(job_b)
+        mx_group(4, 0, pieces=1)
+        quantise(job_a)
+        mx_group(4, 512, pieces=1)
+        quantise(job_b)
+        for m in (5, 6):
             mx_group(m, 0, pieces=1)
-            mx_group(m, 1, pieces=(2 if m == 7 else 1))
+            mx_group(m, 512, pieces=1)
+        mx_group(7, 0, pieces=2)
+        mx_group(7, 512, width=256, pieces=1)
+        mx_group(7, 768, width=256, pieces=2)

from contextlib import ExitStack

import concourse.mybir as mybir
from concourse.masks import make_identity

F32 = mybir.dt.float32
BF16 = mybir.dt.bfloat16
U32 = mybir.dt.uint32
U8 = mybir.dt.uint8
FP8X4 = mybir.dt.float8_e4m3fn_x4
ADD = mybir.AluOpType.add
SIGMOID = mybir.ActivationFunctionType.Sigmoid

P = 128
B, IDIM, HDIM, S = 1024, 512, 1024, 128
NB = B // P
PASSES = 3
ST_SLOTS = ((0, 1), (2, 3, 4, 5), (6, 7))
FLOPS = 2 * B * HDIM * (IDIM + HDIM + 2 * S)


def tile_stackrnn_pa_kernel(tc, x, hidden, stack_top, Wi, bi, Wh, bh, W0, b0, W1, b1, out):
    nc = tc.nc
    with ExitStack() as ctx:
        keep = ctx.enter_context(tc.tile_pool(name="keep", bufs=1))
        psum = ctx.enter_context(tc.psum_pool(name="psum", bufs=8))
        ctx.enter_context(tc.manual_schedule())

        x_sb = keep.tile([P, NB * IDIM], BF16)
        h_sb = keep.tile([P, NB * HDIM], BF16)
        st_sb = keep.tile([P, NB * 2 * S], BF16)
        wi_sb = keep.tile([P, 8 * IDIM], BF16)
        wh_sb = keep.tile([P, 8 * HDIM], BF16)
        w01_raw = keep.tile([P, 2 * 2 * 4 * S], BF16)
        w01_sb = keep.tile([P, 2 * 4 * 2 * S], BF16)
        bias_rows = keep.tile([P, HDIM], BF16)
        ones = keep.tile([P, P], BF16)
        junk = keep.tile([P, 512], BF16)
        ident_f = keep.tile([P, P], F32)
        warm = keep.tile([P, 1], F32)
        stT = keep.tile([P, NB * P * 2], BF16)
        w01T = keep.tile([P, HDIM * 2], BF16)
        bias_bc = keep.tile([P, HDIM], F32)
        a_codes = keep.tile([P, PASSES, B], U32, align_bytes=64)
        a_scales = keep.tile([P, PASSES, B], U8, align_bytes=64)
        w_codes = keep.tile([P, PASSES, HDIM], U32, align_bytes=64)
        w_scales = keep.tile([P, PASSES, HDIM], U8, align_bytes=64)
        pre = keep.tile([P, NB, HDIM], F32)
        xp_sb = keep.tile([P, NB * IDIM // 2], F32)
        hp_sb = keep.tile([P, NB * HDIM // 2], F32)

        nc.vector.memset(ones[:], 1.0)
        nc.vector.memset(junk[:], 0.0)
        nc.vector.memset(bias_rows[:], 0.0)
        nc.vector.memset(warm[:], 0.0)
        make_identity(nc, ident_f[:])

        st_v = stack_top.rearrange("(p t) s k -> p (t s k)", t=NB)
        w0_v = W0.rearrange("(n p t) k -> p n (t k)", n=2, t=4)
        w1_v = W1.rearrange("(n p t) k -> p n (t k)", n=2, t=4)
        w01_r = w01_raw[:].rearrange("p (n s c) -> p n s c", n=2, s=2)
        x_v = x.rearrange("(p t) k -> p (t k)", t=NB)
        h_v = hidden.rearrange("(p t) k -> p (t k)", t=NB)
        wi_v = Wi.rearrange("(g p t) k -> p g (t k)", g=4, t=2)
        wh_v = Wh.rearrange("(g p t) k -> p g (t k)", g=4, t=2)
        wi_t = wi_sb[:].rearrange("p (g c) -> p g c", g=4)

        nc.sync.dma_start(out=w01_r[:, 0, 0, :], in_=w0_v[:, 0, :])
        nc.sync.dma_start(out=w01_r[:, 0, 1, :], in_=w1_v[:, 0, :])
        nc.sync.dma_start(out=st_sb[:, 0:512], in_=st_v[:, 0:512])
        nc.sync.dma_start(out=st_sb[:, 512:2048], in_=st_v[:, 512:2048])
        for r, b_vec in enumerate((bi, bh, b0, b1)):
            nc.scalar.dma_start(out=bias_rows[r : r + 1, :], in_=b_vec.rearrange("(o n) -> o n", o=1))
        nc.scalar.activation(out=warm[:], in_=warm[:], func=SIGMOID)
        nc.sync.dma_start(out=w01_r[:, 1, 0, :], in_=w0_v[:, 1, :])
        nc.sync.dma_start(out=w01_r[:, 1, 1, :], in_=w1_v[:, 1, :])
        for gg in range(2):
            nc.sync.dma_start(out=wi_t[:, 2 * gg : 2 * gg + 2, :], in_=wi_v[:, 2 * gg : 2 * gg + 2, :])
            for g in (2 * gg, 2 * gg + 1):
                nc.sync.dma_start(out=wh_sb[:, g * 2048 : (g + 1) * 2048], in_=wh_v[:, g, :])
        for hh in range(2):
            nc.sync.dma_start(out=x_sb[:, hh * 2048 : (hh + 1) * 2048], in_=x_v[:, hh * 2048 : (hh + 1) * 2048])
            for pr in (2 * hh, 2 * hh + 1):
                nc.sync.dma_start(out=h_sb[:, pr * 2048 : (pr + 1) * 2048], in_=h_v[:, pr * 2048 : (pr + 1) * 2048])

        words = {"s": st_sb[:].bitcast(F32), "v": w01_sb[:].bitcast(F32)}
        mx_words = {("a", 0): xp_sb[:], ("a", 1): hp_sb[:], ("w", 0): wi_sb[:].bitcast(F32), ("w", 1): wh_sb[:].bitcast(F32)}
        raw_words = (x_sb[:].bitcast(F32), h_sb[:].bitcast(F32))
        stT_w = stT[:].bitcast(F32)
        w01T_w = w01T[:].bitcast(F32)
        stT_e = stT[:].rearrange("p (t j e) -> p t j e", t=NB, e=2)
        w01T_e = w01T[:].rearrange("p (n h e) -> p n h e", n=2, e=2)
        out_v = out.rearrange("(p t) h -> p t h", t=NB)
        grouped = {}
        permuted = set()
        banks = {}

        def sources(kind, c, q):
            if kind == "s":
                return [words[kind][:, t * P : (t + 1) * P] for t in ST_SLOTS[q]]
            if kind == "v":
                return [words[kind][:, (4 * q + i) * P : (4 * q + i + 1) * P] for i in range(4)]
            src = mx_words[(kind, min(c, 1))]
            row_words = IDIM // 2 if c == 0 else HDIM // 2
            off = 0 if c == 0 else (c - 1) * 256
            first = [(2 * q + r) * row_words + off for r in range(2)]
            if kind == "a" and (min(c, 1), q) in permuted:
                base = 2 * q * row_words
                first = [base + r * row_words // 2 + off // 2 for r in range(2)]
                return [src[:, f + u * row_words : f + u * row_words + P] for f in first for u in range(2)]
            if kind == "a":
                src = raw_words[min(c, 1)]
            return [src[:, f + u : f + 2 * P : 2] for f in first for u in range(2)]

        def permute(chunk, on_vector=True):
            big = min(chunk[0][1], 1)
            row_words = HDIM // 2 if big else IDIM // 2
            for q in sorted(set(job[2] for job in chunk)):
                permuted.add((big, q))
                words_of = slice(2 * q * row_words, (2 * q + 2) * row_words)
                dst = mx_words[("a", big)][:, words_of].rearrange("p (u b i) -> p b u i", u=2, i=4)
                src = raw_words[big][:, words_of].rearrange("p (b i u) -> p b u i", u=2, i=4)
                if on_vector:
                    nc.vector.tensor_copy(out=dst, in_=src)
                else:
                    nc.scalar.copy(out=dst, in_=src)

        def transposes(job, first, last):
            if first == 0:
                banks[job] = psum.tile([P, 512], F32, tag="bank", name="tbank")
            srcs = sources(*job)
            for i in range(first, last):
                nc.tensor.transpose(banks[job][:, i * P : (i + 1) * P], srcs[i], ident_f[:])

        def copy_out(job, on_vector=False):
            kind, c, q = job
            bank = banks[job]
            if kind == "s":
                slots = ST_SLOTS[q]
                dst, src = stT_w[:, slots[0] * P : (slots[-1] + 1) * P], bank[:, 0 : len(slots) * P]
            elif kind == "v":
                dst = w01T_w[:, q * 512 : (q + 1) * 512].rearrange("p (j t) -> p j t", t=4)
                src = bank[:].rearrange("p (t j) -> p j t", t=4)
            else:
                grouped[job] = keep.tile([P, 1024], BF16, align_bytes=64, name="grp_%s%d%d" % job)
                gw = grouped[job][:].bitcast(F32)
                if kind == "a":
                    dst = gw.rearrange("p (r j u) -> p r j u", r=2, u=2)
                    src = bank[:].rearrange("p (r u j) -> p r j u", r=2, u=2)
                else:
                    dst = gw.rearrange("p (j r u) -> p j r u", r=2, u=2)
                    src = bank[:].rearrange("p (r u j) -> p j r u", r=2, u=2)
            if on_vector:
                nc.vector.tensor_copy(out=dst, in_=src)
            else:
                nc.scalar.copy(out=dst, in_=src)

        def pair_rows(n):
            dst = words["v"][:, n * 512 : (n + 1) * 512].rearrange("p (t s w) -> p s t w", t=4, s=2)
            src = w01_raw[:].bitcast(F32)[:, n * 512 : (n + 1) * 512].rearrange("p (s t w) -> p s t w", s=2, t=4)
            nc.vector.tensor_copy(out=dst, in_=src)

        def quantise(job):
            kind, c, q = job
            codes, scales = (a_codes, a_scales) if kind == "a" else (w_codes, w_scales)
            cols = slice(q * 256, (q + 1) * 256)
            nc.vector.quantize_mx(out=codes[:, c, cols].bitcast(FP8X4), scales=scales[:, c, cols], in_=grouped[job][:])

        def plain_matmul(group, e):
            m, n = group
            if e == 0:
                banks[group] = psum.tile([P, 512], F32, tag="bank", name="pbank")
            nc.tensor.matmul(banks[group][:], lhsT=stT_e[:, m, :, e], rhs=w01T_e[:, n, :, e], start=(e == 0), stop=(e == 1))

        def add_bias(group):
            m, n = group
            cols = slice(n * 512, (n + 1) * 512)
            nc.vector.tensor_tensor(out=pre[:, m, cols], in0=banks[group][:], in1=bias_bc[:, cols], op=ADD)

        def bank_alone(job, on_vector=False):
            transposes(job, 0, len(sources(*job)))
            copy_out(job, on_vector)

        def plain_group(group, with_bias=True):
            plain_matmul(group, 0)
            plain_matmul(group, 1)
            if with_bias:
                add_bias(group)

        def warm_up(count):
            for i in range(count):
                nc.tensor.matmul(warm_bank[:], lhsT=ones[:], rhs=junk[:], start=True, stop=True)

        def finish(m, first_col, last_col):
            cols = slice(first_col, last_col)
            nc.scalar.activation(out=pre[:, m, cols], in_=pre[:, m, cols], func=SIGMOID)
            nc.sync.dma_start(out=out_v[:, m, cols], in_=pre[:, m, cols])

        def mx_group(m, first_col, width=512, pieces=0):
            bank = psum.tile([P, 512], F32, tag="bank", name="mbank")
            rows = slice(m * P, (m + 1) * P)
            cols = slice(first_col, first_col + width)
            for c in range(PASSES):
                nc.tensor.matmul_mx(
                    out=bank[:, 0:width],
                    lhsT=a_codes[:, c, rows].bitcast(FP8X4),
                    lhsT_scale=a_scales[:, c, rows],
                    rhs=w_codes[:, c, cols].bitcast(FP8X4),
                    rhs_scale=w_scales[:, c, cols],
                    start=(c == 0),
                    stop=(c == PASSES - 1),
                )
            step = width // max(pieces, 1)
            for i in range(max(pieces, 1)):
                part = slice(first_col + i * step, first_col + (i + 1) * step)
                nc.vector.tensor_tensor(out=pre[:, m, part], in0=bank[:, i * step : (i + 1) * step], in1=pre[:, m, part], op=ADD)
                if pieces > 0:
                    finish(m, part.start, part.stop)

        warm_bank = psum.tile([P, 512], F32, tag="bank", name="wbank")
        warm_up(6)
        pair_rows(0)
        bank_alone(("v", 0, 0))
        bank_alone(("s", 0, 0), on_vector=True)
        warm_up(1)
        pair_rows(1)
        bank_alone(("s", 0, 1))
        plain_group((0, 0), with_bias=False)
        bank_alone(("s", 0, 2))
        plain_group((1, 0), with_bias=False)
        bias_banks = []
        for n in range(2):
            bias_banks.append(psum.tile([P, 512], F32, tag="bank", name="bbank"))
            nc.tensor.matmul(bias_banks[n][:], lhsT=ones[:], rhs=bias_rows[:, n * 512 : (n + 1) * 512], start=True, stop=True)
        nc.vector.tensor_copy(out=bias_bc[:, 0:512], in_=bias_banks[0][:])
        nc.scalar.copy(out=bias_bc[:, 512:1024], in_=bias_banks[1][:])
        add_bias((0, 0))
        add_bias((1, 0))
        bank_alone(("v", 0, 1))
        plain_group((2, 0))

        groups = [(3, 0), (4, 0), (5, 0)] + [(m, 1) for m in range(6)] + [(6, 0), (6, 1), (7, 0), (7, 1)]
        chunks = []
        for kind in ("w", "a"):
            for hh in range(2):
                chunks.append([(kind, 0, 2 * hh), (kind, 0, 2 * hh + 1)])
                for q in (2 * hh, 2 * hh + 1):
                    chunks.append([(kind, 1, q), (kind, 2, q)])
        EARLY = 9
        plain_group(groups[0])
        gi = 1
        for i in range(EARLY):
            job_a, job_b = chunks[i]
            bank_alone(job_a)
            if i + 2 in (7, 8):
                permute(chunks[i + 2])
            bank_alone(job_b)
            quantise(job_a)
            plain_group(groups[gi])
            gi += 1
            quantise(job_b)
        permute(chunks[9], on_vector=False)
        for m in range(4):
            mx_group(m, 0)
            mx_group(m, 512)
            if m < 3:
                if m < 2:
                    permute(chunks[10 + m])
                finish(m, 0, HDIM)
        for i in range(EARLY, len(chunks)):
            job_a, job_b = chunks[i]
            bank_alone(job_a)
            bank_alone(job_b)
            if i == EARLY + 1:
                finish(3, 0, HDIM)
            plain_group(groups[gi])
            gi += 1
            if i < len(chunks) - 1:
                quantise(job_a)
                quantise(job_b)
        mx_group(4, 0, pieces=1)
        quantise(job_a)
        mx_group(4, 512, pieces=1)
        quantise(job_b)
        for m in (5, 6):
            mx_group(m, 0, pieces=1)
            mx_group(m, 512, pieces=1)
        mx_group(7, 0, pieces=2)
        mx_group(7, 512, width=256, pieces=1)
        mx_group(7, 768, width=256, pieces=2)
